import numpy as np
import ml_dtypes


def mxq(x, axis, fmt="e4m3"):
    dtype, down = {"e4m3": (ml_dtypes.float8_e4m3fn, 7), "e5m2": (ml_dtypes.float8_e5m2, 14)}[fmt]
    v = np.moveaxis(np.asarray(x, np.float32).astype(ml_dtypes.bfloat16).astype(np.float64), axis, -1)
    blocks = v.reshape(v.shape[:-1] + (-1, 32))
    amax = np.abs(blocks).max(-1, keepdims=True)
    byte = np.maximum(np.where(amax > 0, np.frexp(amax)[1] - 1 + 127, 0) - down, 1)
    scale = np.exp2(byte - 127.0)
    codes = (blocks / scale).astype(np.float32).astype(dtype).astype(np.float64)
    return np.moveaxis((codes * scale).reshape(v.shape), -1, axis)


WIDE = False


def mx_kscale(k):
    if not WIDE:
        return np.ones(k)
    levels = np.array([20, -20, 10, -10, 0])
    a = np.random.permutation(np.resize(levels, k // 512 * 4)).reshape(k // 512, 4)
    idx = np.arange(k)
    return np.exp2(a[idx // 512, idx % 128 // 32])


BF16 = ml_dtypes.bfloat16


def bf(x):
    return np.asarray(x, np.float32).astype(BF16)


def f64(x):
    return np.asarray(x).astype(np.float64)


N, CI, CO, H, W, KH, KW = 2, 512, 512, 8, 8, 3, 3
HO, WO = H - KH + 1, W - KW + 1
L = N * HO * WO
K = KH * KW * CI


def setup_inputs():
    u = np.unique(mx_kscale(K))
    s = u[((np.arange(CI) // 32) * (len(u) - 1)) % len(u)][None, :, None, None]
    x = np.random.standard_normal((N, CI, H, W)) * s
    go = np.random.standard_normal((N, CO, HO, WO)) / np.sqrt(L)
    g = np.random.standard_normal((CO, CI, KH, KW)) * np.exp2(np.random.randint(-12, 1, (CO, 1, 1, 1))) * 0.25 / s
    return {"input": bf(x), "grad_output": bf(go), "grad_out": bf(g)}


def reference(input, grad_output, grad_out):
    xq = mxq(f64(input), 1, "e4m3")
    gq = mxq(f64(grad_out), 1, "e5m2")
    a = gq.transpose(0, 2, 3, 1).reshape(CO, K)
    wins = np.stack([xq[:, :, i:i + HO, j:j + WO] for i in range(KH) for j in range(KW)], axis=0)
    b = wins.transpose(0, 2, 1, 3, 4).reshape(K, L)
    y = a @ b
    return np.ascontiguousarray(y.reshape(CO, N, HO, WO).transpose(1, 0, 2, 3))

@@ -1,0 +1,172 @@
+from contextlib import ExitStack
+
+import concourse.mybir as mybir
+from concourse.masks import make_identity
+
+BF16 = mybir.dt.bfloat16
+F32 = mybir.dt.float32
+U32 = mybir.dt.uint32
+U8 = mybir.dt.uint8
+E4M3_X4 = mybir.dt.float8_e4m3fn_x4
+E5M2_X4 = mybir.dt.float8_e5m2_x4
+
+P = 128
+PACK = 4
+PAIR = 2
+WORDS = PACK // PAIR
+
+IMAGES, C_IN, C_OUT = 2, 512, 512
+H, W = 8, 8
+KH, KW = 3, 3
+HO, WO = H - KH + 1, W - KW + 1
+TAPS = KH * KW
+PIXELS = IMAGES * H * W
+ROW = C_IN * TAPS
+O_TILES = C_OUT // P
+assert C_IN == P * PACK and PIXELS == P
+
+X_COLS = PIXELS + (KH - 1) * W
+X_PAD = X_COLS + (KW - 1) - PIXELS
+
+TAPS_PER_UNIT = 2
+UNIT = TAPS_PER_UNIT * C_IN
+
+SCALAR_REGROUPS_TAP = 4
+
+FLOPS = 2 * C_OUT * ROW * IMAGES * HO * WO
+BYTES = 2 * IMAGES * C_IN * H * W + 2 * C_OUT * ROW + 4 * IMAGES * C_OUT * HO * WO
+
+
+def tile_model_pa_s_kernel(tc, x, grad_output, g, out):
+    nc = tc.nc
+    with ExitStack() as ctx:
+        ctx.enter_context(tc.manual_schedule())
+        keep = ctx.enter_context(tc.tile_pool(name="keep", bufs=1))
+        rows_pool = ctx.enter_context(tc.tile_pool(name="rows", bufs=O_TILES))
+        stage = ctx.enter_context(tc.tile_pool(name="stage", bufs=4))
+        banks = ctx.enter_context(tc.psum_pool(name="banks", bufs=6))
+        sums = ctx.enter_context(tc.psum_pool(name="sums", bufs=1))
+
+        x_raw = keep.tile([P, IMAGES, PACK * H * W], BF16)
+        nc.sync.dma_start(out=x_raw[:], in_=x.rearrange("n (p t) h w -> p n (t h w)", t=PACK))
+        g_by_tile = g.rearrange("(r s) c kh kw -> s r (c kh kw)", s=O_TILES)
+        g_rows = []
+        for s in range(O_TILES):
+            rows = rows_pool.tile([P, ROW], BF16, name="g_rows")
+            nc.sync.dma_start(out=rows[:], in_=g_by_tile[s])
+            g_rows.append(rows)
+
+        identity = keep.tile([P, P], F32)
+        make_identity(nc, identity[:])
+
+        x_pixels = keep.tile([P, PIXELS + X_PAD, PACK], BF16)
+        nc.vector.memset(x_pixels[:, PIXELS:, :], 0.0)
+        nc.vector.tensor_copy(
+            out=x_pixels[:, 0:PIXELS, :].rearrange("p (n q) t -> p n q t", n=IMAGES),
+            in_=x_raw[:].rearrange("p n (t q) -> p n q t", t=PACK),
+        )
+        x_codes = keep.tile([P, TAPS, PIXELS], U32, align_bytes=64)
+        x_scales = keep.tile([P, TAPS, PIXELS], U8, align_bytes=64)
+        x_shifted = []
+        for kw in range(KW):
+            shifted = keep.tile([P, X_COLS, PACK], BF16, name="x_shifted%d" % kw, align_bytes=64)
+            nc.vector.tensor_copy(out=shifted[:], in_=x_pixels[:, kw : kw + X_COLS, :])
+            x_shifted.append(shifted)
+        for kh in range(KH):
+            for kw in range(KW):
+                tap = kh * KW + kw
+                nc.vector.quantize_mx(
+                    out=x_codes[:, tap, :].bitcast(E4M3_X4),
+                    scales=x_scales[:, tap, :],
+                    in_=x_shifted[kw][:, kh * W : kh * W + PIXELS, :].rearrange("p q t -> p (q t)"),
+                )
+
+        g_codes = keep.tile([P, TAPS, C_OUT], U32, align_bytes=64)
+        g_scales = keep.tile([P, TAPS, C_OUT], U8, align_bytes=64)
+
+        units = [
+            (s, first_tap, min(TAPS_PER_UNIT, TAPS - first_tap))
+            for s in range(O_TILES)
+            for first_tap in range(0, TAPS, TAPS_PER_UNIT)
+        ]
+        sorted_rows = {}
+        turned = {}
+        grouped = {}
+
+        def regroup(i):
+            s, first_tap, n_taps = units[i]
+            sorted_rows[i] = stage.tile([P, UNIT], BF16, name="sorted_rows")
+            dst = sorted_rows[i][:, 0 : n_taps * C_IN].rearrange(
+                "r (k u p e) -> r k u p e", k=n_taps, u=WORDS, e=PAIR
+            )
+            src = g_rows[s][:].rearrange("r (p u e k) -> r k u p e", u=WORDS, e=PAIR, k=TAPS)
+            if first_tap == SCALAR_REGROUPS_TAP:
+                for k in range(n_taps):
+                    nc.scalar.copy(out=dst[:, k], in_=src[:, first_tap + k])
+            else:
+                nc.vector.tensor_copy(out=dst, in_=src[:, first_tap : first_tap + n_taps])
+
+        def transpose(i):
+            s, first_tap, n_taps = units[i]
+            turned[i] = banks.tile([P, TAPS_PER_UNIT * WORDS * P], F32, name="turned")
+            words = sorted_rows[i][:].bitcast(F32)
+            for plane in range(n_taps * WORDS):
+                cols = slice(plane * P, (plane + 1) * P)
+                nc.tensor.transpose(turned[i][:, cols], words[:, cols], identity[:])
+
+        def copy_out(i):
+            s, first_tap, n_taps = units[i]
+            grouped[i] = stage.tile([P, UNIT], BF16, name="grouped", align_bytes=64)
+            n_words = n_taps * WORDS * P
+            nc.scalar.copy(
+                out=grouped[i][:].bitcast(F32)[:, 0:n_words].rearrange(
+                    "p (k r u) -> p k r u", k=n_taps, u=WORDS
+                ),
+                in_=turned[i][:, 0:n_words].rearrange("p (k u r) -> p k r u", k=n_taps, u=WORDS),
+            )
+
+        def quantise(i):
+            s, first_tap, n_taps = units[i]
+            o_cols = slice(s * P, (s + 1) * P)
+            for k in range(n_taps):
+                nc.vector.quantize_mx(
+                    out=g_codes[:, first_tap + k, o_cols].bitcast(E5M2_X4),
+                    scales=g_scales[:, first_tap + k, o_cols],
+                    in_=grouped[i][:, k * C_IN : (k + 1) * C_IN],
+                )
+
+        stages = [regroup, transpose, copy_out, quantise]
+        for step in range(len(units) + len(stages) - 1):
+            for lag, work in enumerate(stages):
+                if 0 <= step - lag < len(units):
+                    work(step - lag)
+
+        acc = sums.tile([P, C_OUT], F32)
+        for tap in range(TAPS):
+            nc.tensor.matmul_mx(
+                out=acc[:],
+                lhsT=x_codes[:, tap, :].bitcast(E4M3_X4),
+                lhsT_scale=x_scales[:, tap, :],
+                rhs=g_codes[:, tap, :].bitcast(E5M2_X4),
+                rhs_scale=g_scales[:, tap, :],
+                start=(tap == 0),
+                stop=(tap == TAPS - 1),
+            )
+
+        y = keep.tile([P, C_OUT], F32)
+        nc.scalar.copy(out=y[:], in_=acc[:])
+        y_turned = sums.tile([P, O_TILES, PIXELS], F32)
+        for s in range(O_TILES):
+            nc.tensor.transpose(y_turned[:, s, :], y[:, s * P : (s + 1) * P], identity[:])
+        result = keep.tile([P, IMAGES, O_TILES, HO * WO], F32)
+        for n in range(IMAGES):
+            nc.vector.tensor_copy(
+                out=result[:, n].rearrange("r s (i j) -> r s i j", j=WO),
+                in_=y_turned[:, :, n * H * W : (n + 1) * H * W].rearrange(
+                    "r s (h w) -> r s h w", w=W
+                )[:, :, 0:HO, 0:WO],
+            )
+        nc.sync.dma_start(
+            out=out.rearrange("n (r s) i j -> r n (s i j)", s=O_TILES),
+            in_=result[:].rearrange("r n s q -> r n (s q)"),
+        )

@@ -97,14 +97,15 @@ def tile_model_pa_s_kernel(tc, x, grad_output, g, out):
             s, first_tap, n_taps = units[i]
             sorted_rows[i] = stage.tile([P, UNIT], BF16, name="sorted_rows")
             dst = sorted_rows[i][:, 0 : n_taps * C_IN].rearrange(
-                "r (k u p e) -> r k u p e", k=n_taps, u=WORDS, e=PAIR
+                "r (k u p e) -> r u p e k", k=n_taps, u=WORDS, e=PAIR
             )
-            src = g_rows[s][:].rearrange("r (p u e k) -> r k u p e", u=WORDS, e=PAIR, k=TAPS)
+            src = g_rows[s][:].rearrange("r (p u e k) -> r u p e k", u=WORDS, e=PAIR, k=TAPS)
+            src = src[:, :, :, :, first_tap : first_tap + n_taps]
             if first_tap == SCALAR_REGROUPS_TAP:
-                for k in range(n_taps):
-                    nc.scalar.copy(out=dst[:, k], in_=src[:, first_tap + k])
+                for u in range(WORDS):
+                    nc.scalar.copy(out=dst[:, u], in_=src[:, u])
             else:
-                nc.vector.tensor_copy(out=dst, in_=src[:, first_tap : first_tap + n_taps])
+                nc.vector.tensor_copy(out=dst, in_=src)
 
         def transpose(i):
             s, first_tap, n_taps = units[i]

@@ -28,10 +28,10 @@ assert C_IN == P * PACK and PIXELS == P
 X_COLS = PIXELS + (KH - 1) * W
 X_PAD = X_COLS + (KW - 1) - PIXELS
 
-TAPS_PER_UNIT = 2
-UNIT = TAPS_PER_UNIT * C_IN
+UNIT = KW * C_IN
+TAPS_PER_BANK = 2
 
-SCALAR_REGROUPS_TAP = 4
+VECTOR_GROUPS = 104
 
 FLOPS = 2 * C_OUT * ROW * IMAGES * HO * WO
 BYTES = 2 * IMAGES * C_IN * H * W + 2 * C_OUT * ROW + 4 * IMAGES * C_OUT * HO * WO
@@ -44,7 +44,7 @@ def tile_model_pa_s_kernel(tc, x, grad_output, g, out):
         keep = ctx.enter_context(tc.tile_pool(name="keep", bufs=1))
         rows_pool = ctx.enter_context(tc.tile_pool(name="rows", bufs=O_TILES))
         stage = ctx.enter_context(tc.tile_pool(name="stage", bufs=4))
-        banks = ctx.enter_context(tc.psum_pool(name="banks", bufs=6))
+        banks = ctx.enter_context(tc.psum_pool(name="banks", bufs=3))
         sums = ctx.enter_context(tc.psum_pool(name="sums", bufs=1))
 
         x_raw = keep.tile([P, IMAGES, PACK * H * W], BF16)
@@ -84,55 +84,47 @@ def tile_model_pa_s_kernel(tc, x, grad_output, g, out):
         g_codes = keep.tile([P, TAPS, C_OUT], U32, align_bytes=64)
         g_scales = keep.tile([P, TAPS, C_OUT], U8, align_bytes=64)
 
-        units = [
-            (s, first_tap, min(TAPS_PER_UNIT, TAPS - first_tap))
-            for s in range(O_TILES)
-            for first_tap in range(0, TAPS, TAPS_PER_UNIT)
-        ]
+        units = [(s, kh) for s in range(O_TILES) for kh in range(KH)]
         sorted_rows = {}
         turned = {}
         grouped = {}
 
         def regroup(i):
-            s, first_tap, n_taps = units[i]
+            s, kh = units[i]
             sorted_rows[i] = stage.tile([P, UNIT], BF16, name="sorted_rows")
-            dst = sorted_rows[i][:, 0 : n_taps * C_IN].rearrange(
-                "r (k u p e) -> r u p e k", k=n_taps, u=WORDS, e=PAIR
-            )
+            dst = sorted_rows[i][:].rearrange("r (k u p e) -> r u p e k", k=KW, u=WORDS, e=PAIR)
             src = g_rows[s][:].rearrange("r (p u e k) -> r u p e k", u=WORDS, e=PAIR, k=TAPS)
-            src = src[:, :, :, :, first_tap : first_tap + n_taps]
-            if first_tap == SCALAR_REGROUPS_TAP:
-                for u in range(WORDS):
-                    nc.scalar.copy(out=dst[:, u], in_=src[:, u])
-            else:
-                nc.vector.tensor_copy(out=dst, in_=src)
+            src = src[:, :, :, :, kh * KW : (kh + 1) * KW]
+            nc.vector.tensor_copy(out=dst[:, :, 0:VECTOR_GROUPS], in_=src[:, :, 0:VECTOR_GROUPS])
+            for u in range(WORDS):
+                nc.scalar.copy(out=dst[:, u, VECTOR_GROUPS:P], in_=src[:, u, VECTOR_GROUPS:P])
 
         def transpose(i):
-            s, first_tap, n_taps = units[i]
-            turned[i] = banks.tile([P, TAPS_PER_UNIT * WORDS * P], F32, name="turned")
+            turned[i] = banks.tile([P, KW * WORDS * P], F32, name="turned")
             words = sorted_rows[i][:].bitcast(F32)
-            for plane in range(n_taps * WORDS):
+            for plane in range(KW * WORDS):
                 cols = slice(plane * P, (plane + 1) * P)
                 nc.tensor.transpose(turned[i][:, cols], words[:, cols], identity[:])
 
         def copy_out(i):
-            s, first_tap, n_taps = units[i]
             grouped[i] = stage.tile([P, UNIT], BF16, name="grouped", align_bytes=64)
-            n_words = n_taps * WORDS * P
-            nc.scalar.copy(
-                out=grouped[i][:].bitcast(F32)[:, 0:n_words].rearrange(
-                    "p (k r u) -> p k r u", k=n_taps, u=WORDS
-                ),
-                in_=turned[i][:, 0:n_words].rearrange("p (k u r) -> p k r u", k=n_taps, u=WORDS),
-            )
+            for k in range(0, KW, TAPS_PER_BANK):
+                n_taps = min(TAPS_PER_BANK, KW - k)
+                in_bank = slice(k * WORDS * P, (k + n_taps) * WORDS * P)
+                nc.scalar.copy(
+                    out=grouped[i][:].bitcast(F32)[:, in_bank].rearrange(
+                        "p (k r u) -> p k r u", k=n_taps, u=WORDS
+                    ),
+                    in_=turned[i][:, in_bank].rearrange("p (k u r) -> p k r u", k=n_taps, u=WORDS),
+                )
 
         def quantise(i):
-            s, first_tap, n_taps = units[i]
+            s, kh = units[i]
             o_cols = slice(s * P, (s + 1) * P)
-            for k in range(n_taps):
+            for k in range(KW):
                 nc.vector.quantize_mx(
-                    out=g_codes[:, first_tap + k, o_cols].bitcast(E5M2_X4),
-                    scales=g_scales[:, first_tap + k, o_cols],
+                    out=g_codes[:, kh * KW + k, o_cols].bitcast(E5M2_X4),
+                    scales=g_scales[:, kh * KW + k, o_cols],
                     in_=grouped[i][:, k * C_IN : (k + 1) * C_IN],
                 )
 

@@ -30,6 +30,8 @@ X_PAD = X_COLS + (KW - 1) - PIXELS
 
 UNIT = KW * C_IN
 TAPS_PER_BANK = 2
+BANK_F32 = 512
+HALVES = 2
 
 VECTOR_GROUPS = 104
 
@@ -96,11 +98,10 @@ def tile_model_pa_s_kernel(tc, x, grad_output, g, out):
             src = g_rows[s][:].rearrange("r (p u e k) -> r u p e k", u=WORDS, e=PAIR, k=TAPS)
             src = src[:, :, :, :, kh * KW : (kh + 1) * KW]
             nc.vector.tensor_copy(out=dst[:, :, 0:VECTOR_GROUPS], in_=src[:, :, 0:VECTOR_GROUPS])
-            for u in range(WORDS):
-                nc.scalar.copy(out=dst[:, u, VECTOR_GROUPS:P], in_=src[:, u, VECTOR_GROUPS:P])
+            nc.scalar.copy(out=dst[:, :, VECTOR_GROUPS:P], in_=src[:, :, VECTOR_GROUPS:P])
 
         def transpose(i):
-            turned[i] = banks.tile([P, KW * WORDS * P], F32, name="turned")
+            turned[i] = banks.tile([P, HALVES * BANK_F32], F32, name="turned")
             words = sorted_rows[i][:].bitcast(F32)
             for plane in range(KW * WORDS):
                 cols = slice(plane * P, (plane + 1) * P)
@@ -147,19 +148,24 @@ def tile_model_pa_s_kernel(tc, x, grad_output, g, out):
             )
 
         y = keep.tile([P, C_OUT], F32)
-        nc.scalar.copy(out=y[:], in_=acc[:])
-        y_turned = sums.tile([P, O_TILES, PIXELS], F32)
-        for s in range(O_TILES):
-            nc.tensor.transpose(y_turned[:, s, :], y[:, s * P : (s + 1) * P], identity[:])
+        y_banks = banks.tile([P, HALVES * BANK_F32], F32, name="turned")
+        y_turned = y_banks[:].rearrange("r (b c) -> r b c", b=HALVES)
         result = keep.tile([P, IMAGES, O_TILES, HO * WO], F32)
-        for n in range(IMAGES):
-            nc.vector.tensor_copy(
-                out=result[:, n].rearrange("r s (i j) -> r s i j", j=WO),
-                in_=y_turned[:, :, n * H * W : (n + 1) * H * W].rearrange(
-                    "r s (h w) -> r s h w", w=W
-                )[:, :, 0:HO, 0:WO],
-            )
-        nc.sync.dma_start(
-            out=out.rearrange("n (r s) i j -> r n (s i j)", s=O_TILES),
-            in_=result[:].rearrange("r n s q -> r n (s q)"),
-        )
+        out_rows = out.rearrange("n (r s) i j -> r n s (i j)", s=O_TILES)
+        per_half = O_TILES // HALVES
+        for half in range(HALVES):
+            o_cols = slice(half * per_half * P, (half + 1) * per_half * P)
+            nc.scalar.copy(out=y[:, o_cols], in_=acc[:, o_cols])
+        for half in range(HALVES):
+            for j in range(per_half):
+                s = half * per_half + j
+                nc.tensor.transpose(y_turned[:, half, j * P : (j + 1) * P], y[:, s * P : (s + 1) * P], identity[:])
+        for half in range(HALVES):
+            tiles = slice(half * per_half, (half + 1) * per_half)
+            for n in range(IMAGES):
+                dst = result[:, n, tiles, :].rearrange("r s (i j) -> r s i j", j=WO)
+                src = y_turned[:, half, 0 : per_half * P].rearrange(
+                    "r (s n h w) -> r n s h w", s=per_half, n=IMAGES, w=W
+                )[:, n, :, 0:HO, 0:WO]
+                nc.vector.tensor_copy(out=dst, in_=src)
+        nc.sync.dma_start(out=out_rows, in_=result[:])

@@ -162,10 +162,10 @@ def tile_model_pa_s_kernel(tc, x, grad_output, g, out):
                 nc.tensor.transpose(y_turned[:, half, j * P : (j + 1) * P], y[:, s * P : (s + 1) * P], identity[:])
         for half in range(HALVES):
             tiles = slice(half * per_half, (half + 1) * per_half)
-            for n in range(IMAGES):
-                dst = result[:, n, tiles, :].rearrange("r s (i j) -> r s i j", j=WO)
-                src = y_turned[:, half, 0 : per_half * P].rearrange(
+            nc.vector.tensor_copy(
+                out=result[:, :, tiles, :].rearrange("r n s (i j) -> r n s i j", j=WO),
+                in_=y_turned[:, half, 0 : per_half * P].rearrange(
                     "r (s n h w) -> r n s h w", s=per_half, n=IMAGES, w=W
-                )[:, n, :, 0:HO, 0:WO]
-                nc.vector.tensor_copy(out=dst, in_=src)
+                )[:, :, :, 0:HO, 0:WO],
+            )
         nc.sync.dma_start(out=out_rows, in_=result[:])

@@ -33,7 +33,7 @@ TAPS_PER_BANK = 2
 BANK_F32 = 512
 HALVES = 2
 
-VECTOR_GROUPS = 104
+VECTOR_GROUPS = 100
 
 FLOPS = 2 * C_OUT * ROW * IMAGES * HO * WO
 BYTES = 2 * IMAGES * C_IN * H * W + 2 * C_OUT * ROW + 4 * IMAGES * C_OUT * HO * WO

@@ -33,7 +33,9 @@ TAPS_PER_BANK = 2
 BANK_F32 = 512
 HALVES = 2
 
-VECTOR_GROUPS = 100
+VECTOR_GROUPS = 104
+HALVED = 2
+HALF_GROUPS = P // 2
 
 FLOPS = 2 * C_OUT * ROW * IMAGES * HO * WO
 BYTES = 2 * IMAGES * C_IN * H * W + 2 * C_OUT * ROW + 4 * IMAGES * C_OUT * HO * WO
@@ -55,7 +57,10 @@ def tile_model_pa_s_kernel(tc, x, grad_output, g, out):
         g_rows = []
         for s in range(O_TILES):
             rows = rows_pool.tile([P, ROW], BF16, name="g_rows")
-            nc.sync.dma_start(out=rows[:], in_=g_by_tile[s])
+            parts = 2 if s < HALVED else 1
+            for part in range(parts):
+                cols = slice(part * ROW // parts, (part + 1) * ROW // parts)
+                nc.sync.dma_start(out=rows[:, cols], in_=g_by_tile[s][:, cols])
             g_rows.append(rows)
 
         identity = keep.tile([P, P], F32)
@@ -91,14 +96,27 @@ def tile_model_pa_s_kernel(tc, x, grad_output, g, out):
         turned = {}
         grouped = {}
 
-        def regroup(i):
+        def regroup_groups(copy, i, groups):
             s, kh = units[i]
-            sorted_rows[i] = stage.tile([P, UNIT], BF16, name="sorted_rows")
+            if i not in sorted_rows:
+                sorted_rows[i] = stage.tile([P, UNIT], BF16, name="sorted_rows", bufs=6)
             dst = sorted_rows[i][:].rearrange("r (k u p e) -> r u p e k", k=KW, u=WORDS, e=PAIR)
             src = g_rows[s][:].rearrange("r (p u e k) -> r u p e k", u=WORDS, e=PAIR, k=TAPS)
             src = src[:, :, :, :, kh * KW : (kh + 1) * KW]
-            nc.vector.tensor_copy(out=dst[:, :, 0:VECTOR_GROUPS], in_=src[:, :, 0:VECTOR_GROUPS])
-            nc.scalar.copy(out=dst[:, :, VECTOR_GROUPS:P], in_=src[:, :, VECTOR_GROUPS:P])
+            copy(out=dst[:, :, groups], in_=src[:, :, groups])
+
+        def regroup(i):
+            s, kh = units[i]
+            if s == 0:
+                regroup_groups(nc.scalar.copy, i, slice(0, HALF_GROUPS))
+                regroup_groups(nc.vector.tensor_copy, i, slice(HALF_GROUPS, P))
+                return
+            if s < HALVED and kh == 0:
+                for j in range(i, i + KH):
+                    regroup_groups(nc.vector.tensor_copy, j, slice(0, HALF_GROUPS))
+            done = HALF_GROUPS if s < HALVED else 0
+            regroup_groups(nc.vector.tensor_copy, i, slice(done, VECTOR_GROUPS))
+            regroup_groups(nc.scalar.copy, i, slice(VECTOR_GROUPS, P))
 
         def transpose(i):
             turned[i] = banks.tile([P, HALVES * BANK_F32], F32, name="turned")

@@ -36,6 +36,7 @@ HALVES = 2
 VECTOR_GROUPS = 104
 HALVED = 2
 HALF_GROUPS = P // 2
+BUSY_PASSES = 2
 
 FLOPS = 2 * C_OUT * ROW * IMAGES * HO * WO
 BYTES = 2 * IMAGES * C_IN * H * W + 2 * C_OUT * ROW + 4 * IMAGES * C_OUT * HO * WO
@@ -147,11 +148,27 @@ def tile_model_pa_s_kernel(tc, x, grad_output, g, out):
                     in_=grouped[i][:, k * C_IN : (k + 1) * C_IN],
                 )
 
+        idle_sum = sums.tile([P, C_OUT], F32)
+
+        def keep_busy():
+            nc.tensor.matmul_mx(
+                out=idle_sum[:],
+                lhsT=g_codes[:, 0, 0:P].bitcast(E5M2_X4),
+                lhsT_scale=g_scales[:, 0, 0:P],
+                rhs=x_codes[:, 0 : C_OUT // PIXELS, :].rearrange("p k q -> p (k q)").bitcast(E4M3_X4),
+                rhs_scale=x_scales[:, 0 : C_OUT // PIXELS, :].rearrange("p k q -> p (k q)"),
+                start=True,
+                stop=True,
+            )
+
         stages = [regroup, transpose, copy_out, quantise]
         for step in range(len(units) + len(stages) - 1):
             for lag, work in enumerate(stages):
                 if 0 <= step - lag < len(units):
                     work(step - lag)
+            if len(stages) <= step < len(units):
+                for i in range(BUSY_PASSES):
+                    keep_busy()
 
         acc = sums.tile([P, C_OUT], F32)
         for tap in range(TAPS):

@@ -36,7 +36,7 @@ HALVES = 2
 VECTOR_GROUPS = 104
 HALVED = 2
 HALF_GROUPS = P // 2
-BUSY_PASSES = 2
+BUSY_PASSES = 1
 
 FLOPS = 2 * C_OUT * ROW * IMAGES * HO * WO
 BYTES = 2 * IMAGES * C_IN * H * W + 2 * C_OUT * ROW + 4 * IMAGES * C_OUT * HO * WO

@@ -36,7 +36,9 @@ HALVES = 2
 VECTOR_GROUPS = 104
 HALVED = 2
 HALF_GROUPS = P // 2
-BUSY_PASSES = 1
+
+SIDE_TILE, SIDE_KH = O_TILES - 1, 0
+MAIN_COLS = SIDE_TILE * P
 
 FLOPS = 2 * C_OUT * ROW * IMAGES * HO * WO
 BYTES = 2 * IMAGES * C_IN * H * W + 2 * C_OUT * ROW + 4 * IMAGES * C_OUT * HO * WO
@@ -49,7 +51,7 @@ def tile_model_pa_s_kernel(tc, x, grad_output, g, out):
         keep = ctx.enter_context(tc.tile_pool(name="keep", bufs=1))
         rows_pool = ctx.enter_context(tc.tile_pool(name="rows", bufs=O_TILES))
         stage = ctx.enter_context(tc.tile_pool(name="stage", bufs=4))
-        banks = ctx.enter_context(tc.psum_pool(name="banks", bufs=3))
+        banks = ctx.enter_context(tc.psum_pool(name="banks", bufs=1))
         sums = ctx.enter_context(tc.psum_pool(name="sums", bufs=1))
 
         x_raw = keep.tile([P, IMAGES, PACK * H * W], BF16)
@@ -91,8 +93,15 @@ def tile_model_pa_s_kernel(tc, x, grad_output, g, out):
 
         g_codes = keep.tile([P, TAPS, C_OUT], U32, align_bytes=64)
         g_scales = keep.tile([P, TAPS, C_OUT], U8, align_bytes=64)
+        side_codes = keep.tile([P, KW, P], U32, align_bytes=64)
+        side_scales = keep.tile([P, KW, P], U8, align_bytes=64)
+        side_taps = slice(SIDE_KH * KW, (SIDE_KH + 1) * KW)
+        nc.gpsimd.memset(g_codes[:, side_taps, MAIN_COLS:], 0)
+        nc.gpsimd.memset(g_scales[:, side_taps, MAIN_COLS:].bitcast(U32), 0)
 
         units = [(s, kh) for s in range(O_TILES) for kh in range(KH)]
+        units.remove((SIDE_TILE, SIDE_KH))
+        units.append((SIDE_TILE, SIDE_KH))
         sorted_rows = {}
         turned = {}
         grouped = {}
@@ -120,39 +129,44 @@ def tile_model_pa_s_kernel(tc, x, grad_output, g, out):
             regroup_groups(nc.scalar.copy, i, slice(VECTOR_GROUPS, P))
 
         def transpose(i):
-            turned[i] = banks.tile([P, HALVES * BANK_F32], F32, name="turned")
+            two_taps = banks.tile([P, BANK_F32], F32, name="two_taps", bufs=4)
+            one_tap = banks.tile([P, BANK_F32], F32, name="one_tap", bufs=3)
+            turned[i] = [two_taps, one_tap]
             words = sorted_rows[i][:].bitcast(F32)
             for plane in range(KW * WORDS):
-                cols = slice(plane * P, (plane + 1) * P)
-                nc.tensor.transpose(turned[i][:, cols], words[:, cols], identity[:])
+                bank, slot = divmod(plane, TAPS_PER_BANK * WORDS)
+                nc.tensor.transpose(
+                    turned[i][bank][:, slot * P : (slot + 1) * P], words[:, plane * P : (plane + 1) * P], identity[:]
+                )
 
         def copy_out(i):
             grouped[i] = stage.tile([P, UNIT], BF16, name="grouped", align_bytes=64)
-            for k in range(0, KW, TAPS_PER_BANK):
+            for bank, k in enumerate(range(0, KW, TAPS_PER_BANK)):
                 n_taps = min(TAPS_PER_BANK, KW - k)
-                in_bank = slice(k * WORDS * P, (k + n_taps) * WORDS * P)
+                out_elements = grouped[i][:, k * C_IN : (k + n_taps) * C_IN]
+                in_words = turned[i][bank][:, 0 : n_taps * WORDS * P]
                 nc.scalar.copy(
-                    out=grouped[i][:].bitcast(F32)[:, in_bank].rearrange(
-                        "p (k r u) -> p k r u", k=n_taps, u=WORDS
-                    ),
-                    in_=turned[i][:, in_bank].rearrange("p (k u r) -> p k r u", k=n_taps, u=WORDS),
+                    out=out_elements.bitcast(F32).rearrange("p (k r u) -> p k r u", k=n_taps, u=WORDS),
+                    in_=in_words.rearrange("p (k u r) -> p k r u", k=n_taps, u=WORDS),
                 )
 
         def quantise(i):
             s, kh = units[i]
             o_cols = slice(s * P, (s + 1) * P)
             for k in range(KW):
+                if (s, kh) == (SIDE_TILE, SIDE_KH):
+                    codes, scales = side_codes[:, k, :], side_scales[:, k, :]
+                else:
+                    codes, scales = g_codes[:, kh * KW + k, o_cols], g_scales[:, kh * KW + k, o_cols]
                 nc.vector.quantize_mx(
-                    out=g_codes[:, kh * KW + k, o_cols].bitcast(E5M2_X4),
-                    scales=g_scales[:, kh * KW + k, o_cols],
-                    in_=grouped[i][:, k * C_IN : (k + 1) * C_IN],
+                    out=codes.bitcast(E5M2_X4), scales=scales, in_=grouped[i][:, k * C_IN : (k + 1) * C_IN]
                 )
 
-        idle_sum = sums.tile([P, C_OUT], F32)
+        acc = sums.tile([P, C_OUT], F32)
 
         def keep_busy():
             nc.tensor.matmul_mx(
-                out=idle_sum[:],
+                out=acc[:],
                 lhsT=g_codes[:, 0, 0:P].bitcast(E5M2_X4),
                 lhsT_scale=g_scales[:, 0, 0:P],
                 rhs=x_codes[:, 0 : C_OUT // PIXELS, :].rearrange("p k q -> p (k q)").bitcast(E4M3_X4),
@@ -161,46 +175,75 @@ def tile_model_pa_s_kernel(tc, x, grad_output, g, out):
                 stop=True,
             )
 
-        stages = [regroup, transpose, copy_out, quantise]
-        for step in range(len(units) + len(stages) - 1):
-            for lag, work in enumerate(stages):
-                if 0 <= step - lag < len(units):
-                    work(step - lag)
-            if len(stages) <= step < len(units):
-                for i in range(BUSY_PASSES):
-                    keep_busy()
+        main_taps = list(range(SIDE_KH * KW, (SIDE_KH + 1) * KW))
+        main_taps += [tap for tap in range(TAPS) if tap not in main_taps]
 
-        acc = sums.tile([P, C_OUT], F32)
-        for tap in range(TAPS):
+        def main_pass(tap):
             nc.tensor.matmul_mx(
                 out=acc[:],
                 lhsT=x_codes[:, tap, :].bitcast(E4M3_X4),
                 lhsT_scale=x_scales[:, tap, :],
                 rhs=g_codes[:, tap, :].bitcast(E5M2_X4),
                 rhs_scale=g_scales[:, tap, :],
-                start=(tap == 0),
-                stop=(tap == TAPS - 1),
+                start=(tap == main_taps[0]),
+                stop=(tap == main_taps[-1]),
+            )
+
+        stages = [regroup, transpose, copy_out, quantise]
+        n = len(units)
+        for step in range(n + len(stages) - 1):
+            for lag, work in enumerate(stages):
+                if 0 <= step - lag < n:
+                    work(step - lag)
+            early = step - (n + 1 - KW)
+            if 0 <= early < KW:
+                main_pass(main_taps[early])
+            elif len(stages) <= step < n:
+                keep_busy()
+        for tap in main_taps[KW:]:
+            main_pass(tap)
+
+        side_sum = banks.tile([P, BANK_F32], F32, name="one_tap", bufs=3)
+        for k in range(KW):
+            windows = slice(SIDE_KH * KW + k, SIDE_KH * KW + k + C_OUT // PIXELS)
+            nc.tensor.matmul_mx(
+                out=side_sum[:],
+                lhsT=side_codes[:, k, :].bitcast(E5M2_X4),
+                lhsT_scale=side_scales[:, k, :],
+                rhs=x_codes[:, windows, :].rearrange("p k q -> p (k q)").bitcast(E4M3_X4),
+                rhs_scale=x_scales[:, windows, :].rearrange("p k q -> p (k q)"),
+                start=(k == 0),
+                stop=(k == KW - 1),
             )
 
         y = keep.tile([P, C_OUT], F32)
-        y_banks = banks.tile([P, HALVES * BANK_F32], F32, name="turned")
-        y_turned = y_banks[:].rearrange("r (b c) -> r b c", b=HALVES)
+        y_turned = []
+        halves = (1, 0)
+        for half in range(HALVES):
+            y_turned.append(banks.tile([P, BANK_F32], F32, name="two_taps", bufs=4))
         result = keep.tile([P, IMAGES, O_TILES, HO * WO], F32)
         out_rows = out.rearrange("n (r s) i j -> r n s (i j)", s=O_TILES)
         per_half = O_TILES // HALVES
-        for half in range(HALVES):
+        for half in halves:
             o_cols = slice(half * per_half * P, (half + 1) * per_half * P)
             nc.scalar.copy(out=y[:, o_cols], in_=acc[:, o_cols])
-        for half in range(HALVES):
+        for half in halves:
             for j in range(per_half):
                 s = half * per_half + j
-                nc.tensor.transpose(y_turned[:, half, j * P : (j + 1) * P], y[:, s * P : (s + 1) * P], identity[:])
-        for half in range(HALVES):
+                nc.tensor.transpose(y_turned[half][:, j * P : (j + 1) * P], y[:, s * P : (s + 1) * P], identity[:])
+        for half in halves:
             tiles = slice(half * per_half, (half + 1) * per_half)
             nc.vector.tensor_copy(
                 out=result[:, :, tiles, :].rearrange("r n s (i j) -> r n s i j", j=WO),
-                in_=y_turned[:, half, 0 : per_half * P].rearrange(
+                in_=y_turned[half][:, 0 : per_half * P].rearrange(
                     "r (s n h w) -> r n s h w", s=per_half, n=IMAGES, w=W
                 )[:, :, :, 0:HO, 0:WO],
             )
+        of_tile = result[:, :, SIDE_TILE, :].rearrange("r n (i j) -> r n i j", j=WO)
+        nc.vector.tensor_tensor(
+            out=of_tile,
+            in0=side_sum[:, 0:PIXELS].rearrange("r (n h w) -> r n h w", n=IMAGES, w=W)[:, :, 0:HO, 0:WO],
+            in1=of_tile,
+            op=mybir.AluOpType.add,
+        )
         nc.sync.dma_start(out=out_rows, in_=result[:])

@@ -69,7 +69,7 @@ def tile_model_pa_s_kernel(tc, x, grad_output, g, out):
         identity = keep.tile([P, P], F32)
         make_identity(nc, identity[:])
 
-        x_pixels = keep.tile([P, PIXELS + X_PAD, PACK], BF16)
+        x_pixels = keep.tile([P, PIXELS + X_PAD, PACK], BF16, align_bytes=64)
         nc.vector.memset(x_pixels[:, PIXELS:, :], 0.0)
         nc.vector.tensor_copy(
             out=x_pixels[:, 0:PIXELS, :].rearrange("p (n q) t -> p n q t", n=IMAGES),
@@ -77,13 +77,13 @@ def tile_model_pa_s_kernel(tc, x, grad_output, g, out):
         )
         x_codes = keep.tile([P, TAPS, PIXELS], U32, align_bytes=64)
         x_scales = keep.tile([P, TAPS, PIXELS], U8, align_bytes=64)
-        x_shifted = []
-        for kw in range(KW):
+        x_shifted = [x_pixels]
+        for kw in range(1, KW):
             shifted = keep.tile([P, X_COLS, PACK], BF16, name="x_shifted%d" % kw, align_bytes=64)
             nc.vector.tensor_copy(out=shifted[:], in_=x_pixels[:, kw : kw + X_COLS, :])
             x_shifted.append(shifted)
-        for kh in range(KH):
-            for kw in range(KW):
+        for kw in range(KW):
+            for kh in range(KH):
                 tap = kh * KW + kw
                 nc.vector.quantize_mx(
                     out=x_codes[:, tap, :].bitcast(E4M3_X4),
@@ -195,9 +195,11 @@ def tile_model_pa_s_kernel(tc, x, grad_output, g, out):
             for lag, work in enumerate(stages):
                 if 0 <= step - lag < n:
                     work(step - lag)
-            early = step - (n + 1 - KW)
-            if 0 <= early < KW:
-                main_pass(main_taps[early])
+            if step == n - 2:
+                main_pass(main_taps[0])
+            elif step == n - 1:
+                main_pass(main_taps[1])
+                main_pass(main_taps[2])
             elif len(stages) <= step < n:
                 keep_busy()
         for tap in main_taps[KW:]:

@@ -33,7 +33,7 @@ TAPS_PER_BANK = 2
 BANK_F32 = 512
 HALVES = 2
 
-VECTOR_GROUPS = 104
+VECTOR_GROUPS = 107
 HALVED = 2
 HALF_GROUPS = P // 2
 

from contextlib import ExitStack

import concourse.mybir as mybir
from concourse.masks import make_identity

BF16 = mybir.dt.bfloat16
F32 = mybir.dt.float32
U32 = mybir.dt.uint32
U8 = mybir.dt.uint8
E4M3_X4 = mybir.dt.float8_e4m3fn_x4
E5M2_X4 = mybir.dt.float8_e5m2_x4

P = 128
PACK = 4
PAIR = 2
WORDS = PACK // PAIR

IMAGES, C_IN, C_OUT = 2, 512, 512
H, W = 8, 8
KH, KW = 3, 3
HO, WO = H - KH + 1, W - KW + 1
TAPS = KH * KW
PIXELS = IMAGES * H * W
ROW = C_IN * TAPS
O_TILES = C_OUT // P
assert C_IN == P * PACK and PIXELS == P

X_COLS = PIXELS + (KH - 1) * W
X_PAD = X_COLS + (KW - 1) - PIXELS

UNIT = KW * C_IN
TAPS_PER_BANK = 2
BANK_F32 = 512
HALVES = 2

VECTOR_GROUPS = 107
HALVED = 2
HALF_GROUPS = P // 2

SIDE_TILE, SIDE_KH = O_TILES - 1, 0
MAIN_COLS = SIDE_TILE * P

FLOPS = 2 * C_OUT * ROW * IMAGES * HO * WO
BYTES = 2 * IMAGES * C_IN * H * W + 2 * C_OUT * ROW + 4 * IMAGES * C_OUT * HO * WO


def tile_model_pa_s_kernel(tc, x, grad_output, g, out):
    nc = tc.nc
    with ExitStack() as ctx:
        ctx.enter_context(tc.manual_schedule())
        keep = ctx.enter_context(tc.tile_pool(name="keep", bufs=1))
        rows_pool = ctx.enter_context(tc.tile_pool(name="rows", bufs=O_TILES))
        stage = ctx.enter_context(tc.tile_pool(name="stage", bufs=4))
        banks = ctx.enter_context(tc.psum_pool(name="banks", bufs=1))
        sums = ctx.enter_context(tc.psum_pool(name="sums", bufs=1))

        x_raw = keep.tile([P, IMAGES, PACK * H * W], BF16)
        nc.sync.dma_start(out=x_raw[:], in_=x.rearrange("n (p t) h w -> p n (t h w)", t=PACK))
        g_by_tile = g.rearrange("(r s) c kh kw -> s r (c kh kw)", s=O_TILES)
        g_rows = []
        for s in range(O_TILES):
            rows = rows_pool.tile([P, ROW], BF16, name="g_rows")
            parts = 2 if s < HALVED else 1
            for part in range(parts):
                cols = slice(part * ROW // parts, (part + 1) * ROW // parts)
                nc.sync.dma_start(out=rows[:, cols], in_=g_by_tile[s][:, cols])
            g_rows.append(rows)

        identity = keep.tile([P, P], F32)
        make_identity(nc, identity[:])

        x_pixels = keep.tile([P, PIXELS + X_PAD, PACK], BF16, align_bytes=64)
        nc.vector.memset(x_pixels[:, PIXELS:, :], 0.0)
        nc.vector.tensor_copy(
            out=x_pixels[:, 0:PIXELS, :].rearrange("p (n q) t -> p n q t", n=IMAGES),
            in_=x_raw[:].rearrange("p n (t q) -> p n q t", t=PACK),
        )
        x_codes = keep.tile([P, TAPS, PIXELS], U32, align_bytes=64)
        x_scales = keep.tile([P, TAPS, PIXELS], U8, align_bytes=64)
        x_shifted = [x_pixels]
        for kw in range(1, KW):
            shifted = keep.tile([P, X_COLS, PACK], BF16, name="x_shifted%d" % kw, align_bytes=64)
            nc.vector.tensor_copy(out=shifted[:], in_=x_pixels[:, kw : kw + X_COLS, :])
            x_shifted.append(shifted)
        for kw in range(KW):
            for kh in range(KH):
                tap = kh * KW + kw
                nc.vector.quantize_mx(
                    out=x_codes[:, tap, :].bitcast(E4M3_X4),
                    scales=x_scales[:, tap, :],
                    in_=x_shifted[kw][:, kh * W : kh * W + PIXELS, :].rearrange("p q t -> p (q t)"),
                )

        g_codes = keep.tile([P, TAPS, C_OUT], U32, align_bytes=64)
        g_scales = keep.tile([P, TAPS, C_OUT], U8, align_bytes=64)
        side_codes = keep.tile([P, KW, P], U32, align_bytes=64)
        side_scales = keep.tile([P, KW, P], U8, align_bytes=64)
        side_taps = slice(SIDE_KH * KW, (SIDE_KH + 1) * KW)
        nc.gpsimd.memset(g_codes[:, side_taps, MAIN_COLS:], 0)
        nc.gpsimd.memset(g_scales[:, side_taps, MAIN_COLS:].bitcast(U32), 0)

        units = [(s, kh) for s in range(O_TILES) for kh in range(KH)]
        units.remove((SIDE_TILE, SIDE_KH))
        units.append((SIDE_TILE, SIDE_KH))
        sorted_rows = {}
        turned = {}
        grouped = {}

        def regroup_groups(copy, i, groups):
            s, kh = units[i]
            if i not in sorted_rows:
                sorted_rows[i] = stage.tile([P, UNIT], BF16, name="sorted_rows", bufs=6)
            dst = sorted_rows[i][:].rearrange("r (k u p e) -> r u p e k", k=KW, u=WORDS, e=PAIR)
            src = g_rows[s][:].rearrange("r (p u e k) -> r u p e k", u=WORDS, e=PAIR, k=TAPS)
            src = src[:, :, :, :, kh * KW : (kh + 1) * KW]
            copy(out=dst[:, :, groups], in_=src[:, :, groups])

        def regroup(i):
            s, kh = units[i]
            if s == 0:
                regroup_groups(nc.scalar.copy, i, slice(0, HALF_GROUPS))
                regroup_groups(nc.vector.tensor_copy, i, slice(HALF_GROUPS, P))
                return
            if s < HALVED and kh == 0:
                for j in range(i, i + KH):
                    regroup_groups(nc.vector.tensor_copy, j, slice(0, HALF_GROUPS))
            done = HALF_GROUPS if s < HALVED else 0
            regroup_groups(nc.vector.tensor_copy, i, slice(done, VECTOR_GROUPS))
            regroup_groups(nc.scalar.copy, i, slice(VECTOR_GROUPS, P))

        def transpose(i):
            two_taps = banks.tile([P, BANK_F32], F32, name="two_taps", bufs=4)
            one_tap = banks.tile([P, BANK_F32], F32, name="one_tap", bufs=3)
            turned[i] = [two_taps, one_tap]
            words = sorted_rows[i][:].bitcast(F32)
            for plane in range(KW * WORDS):
                bank, slot = divmod(plane, TAPS_PER_BANK * WORDS)
                nc.tensor.transpose(
                    turned[i][bank][:, slot * P : (slot + 1) * P], words[:, plane * P : (plane + 1) * P], identity[:]
                )

        def copy_out(i):
            grouped[i] = stage.tile([P, UNIT], BF16, name="grouped", align_bytes=64)
            for bank, k in enumerate(range(0, KW, TAPS_PER_BANK)):
                n_taps = min(TAPS_PER_BANK, KW - k)
                out_elements = grouped[i][:, k * C_IN : (k + n_taps) * C_IN]
                in_words = turned[i][bank][:, 0 : n_taps * WORDS * P]
                nc.scalar.copy(
                    out=out_elements.bitcast(F32).rearrange("p (k r u) -> p k r u", k=n_taps, u=WORDS),
                    in_=in_words.rearrange("p (k u r) -> p k r u", k=n_taps, u=WORDS),
                )

        def quantise(i):
            s, kh = units[i]
            o_cols = slice(s * P, (s + 1) * P)
            for k in range(KW):
                if (s, kh) == (SIDE_TILE, SIDE_KH):
                    codes, scales = side_codes[:, k, :], side_scales[:, k, :]
                else:
                    codes, scales = g_codes[:, kh * KW + k, o_cols], g_scales[:, kh * KW + k, o_cols]
                nc.vector.quantize_mx(
                    out=codes.bitcast(E5M2_X4), scales=scales, in_=grouped[i][:, k * C_IN : (k + 1) * C_IN]
                )

        acc = sums.tile([P, C_OUT], F32)

        def keep_busy():
            nc.tensor.matmul_mx(
                out=acc[:],
                lhsT=g_codes[:, 0, 0:P].bitcast(E5M2_X4),
                lhsT_scale=g_scales[:, 0, 0:P],
                rhs=x_codes[:, 0 : C_OUT // PIXELS, :].rearrange("p k q -> p (k q)").bitcast(E4M3_X4),
                rhs_scale=x_scales[:, 0 : C_OUT // PIXELS, :].rearrange("p k q -> p (k q)"),
                start=True,
                stop=True,
            )

        main_taps = list(range(SIDE_KH * KW, (SIDE_KH + 1) * KW))
        main_taps += [tap for tap in range(TAPS) if tap not in main_taps]

        def main_pass(tap):
            nc.tensor.matmul_mx(
                out=acc[:],
                lhsT=x_codes[:, tap, :].bitcast(E4M3_X4),
                lhsT_scale=x_scales[:, tap, :],
                rhs=g_codes[:, tap, :].bitcast(E5M2_X4),
                rhs_scale=g_scales[:, tap, :],
                start=(tap == main_taps[0]),
                stop=(tap == main_taps[-1]),
            )

        stages = [regroup, transpose, copy_out, quantise]
        n = len(units)
        for step in range(n + len(stages) - 1):
            for lag, work in enumerate(stages):
                if 0 <= step - lag < n:
                    work(step - lag)
            if step == n - 2:
                main_pass(main_taps[0])
            elif step == n - 1:
                main_pass(main_taps[1])
                main_pass(main_taps[2])
            elif len(stages) <= step < n:
                keep_busy()
        for tap in main_taps[KW:]:
            main_pass(tap)

        side_sum = banks.tile([P, BANK_F32], F32, name="one_tap", bufs=3)
        for k in range(KW):
            windows = slice(SIDE_KH * KW + k, SIDE_KH * KW + k + C_OUT // PIXELS)
            nc.tensor.matmul_mx(
                out=side_sum[:],
                lhsT=side_codes[:, k, :].bitcast(E5M2_X4),
                lhsT_scale=side_scales[:, k, :],
                rhs=x_codes[:, windows, :].rearrange("p k q -> p (k q)").bitcast(E4M3_X4),
                rhs_scale=x_scales[:, windows, :].rearrange("p k q -> p (k q)"),
                start=(k == 0),
                stop=(k == KW - 1),
            )

        y = keep.tile([P, C_OUT], F32)
        y_turned = []
        halves = (1, 0)
        for half in range(HALVES):
            y_turned.append(banks.tile([P, BANK_F32], F32, name="two_taps", bufs=4))
        result = keep.tile([P, IMAGES, O_TILES, HO * WO], F32)
        out_rows = out.rearrange("n (r s) i j -> r n s (i j)", s=O_TILES)
        per_half = O_TILES // HALVES
        for half in halves:
            o_cols = slice(half * per_half * P, (half + 1) * per_half * P)
            nc.scalar.copy(out=y[:, o_cols], in_=acc[:, o_cols])
        for half in halves:
            for j in range(per_half):
                s = half * per_half + j
                nc.tensor.transpose(y_turned[half][:, j * P : (j + 1) * P], y[:, s * P : (s + 1) * P], identity[:])
        for half in halves:
            tiles = slice(half * per_half, (half + 1) * per_half)
            nc.vector.tensor_copy(
                out=result[:, :, tiles, :].rearrange("r n s (i j) -> r n s i j", j=WO),
                in_=y_turned[half][:, 0 : per_half * P].rearrange(
                    "r (s n h w) -> r n s h w", s=per_half, n=IMAGES, w=W
                )[:, :, :, 0:HO, 0:WO],
            )
        of_tile = result[:, :, SIDE_TILE, :].rearrange("r n (i j) -> r n i j", j=WO)
        nc.vector.tensor_tensor(
            out=of_tile,
            in0=side_sum[:, 0:PIXELS].rearrange("r (n h w) -> r n h w", n=IMAGES, w=W)[:, :, 0:HO, 0:WO],
            in1=of_tile,
            op=mybir.AluOpType.add,
        )
        nc.sync.dma_start(out=out_rows, in_=result[:])
